import numpy as np
import ml_dtypes


def mxq(x, axis, fmt="e4m3"):
    dtype, down = {"e4m3": (ml_dtypes.float8_e4m3fn, 7), "e5m2": (ml_dtypes.float8_e5m2, 14)}[fmt]
    v = np.moveaxis(np.asarray(x, np.float32).astype(ml_dtypes.bfloat16).astype(np.float64), axis, -1)
    blocks = v.reshape(v.shape[:-1] + (-1, 32))
    amax = np.abs(blocks).max(-1, keepdims=True)
    byte = np.maximum(np.where(amax > 0, np.frexp(amax)[1] - 1 + 127, 0) - down, 1)
    scale = np.exp2(byte - 127.0)
    codes = (blocks / scale).astype(np.float32).astype(dtype).astype(np.float64)
    return np.moveaxis((codes * scale).reshape(v.shape), -1, axis)


WIDE = False


def mx_kscale(k):
    if not WIDE:
        return np.ones(k)
    levels = np.array([10, -10, 5, -5, 0])
    a = np.random.permutation(np.resize(levels, k // 512 * 4)).reshape(k // 512, 4)
    idx = np.arange(k)
    return np.exp2(a[idx // 512, idx % 128 // 32])


BF16 = ml_dtypes.bfloat16


def bf(x):
    return np.asarray(x, np.float32).astype(BF16)


def f64(x):
    return np.asarray(x).astype(np.float64)


B, C, D, T, H, W, P = 1, 1024, 512, 8, 16, 16, 2
N = T * H * W
NP = T * (H // P) * (W // P)


def conv1x1(wq, b, xq):
    return ((wq @ xq) + b[None, :, None]).reshape(B, D, T, H, W)


def maxpool(v):
    return v.reshape(B, D, T, H // P, P, W // P, P).max(axis=(4, 6))


def setup_inputs():
    s = mx_kscale(C)
    a = 1.0 / np.sqrt(C) / s[None, :]
    return {"x": bf(np.random.standard_normal((B, C, T, H, W)) * s[None, :, None, None, None]),
            "g_w": bf(np.random.standard_normal((D, C)) * 0.15 * a),
            "g_b": bf(np.random.standard_normal(D) * 0.03),
            "theta_w": bf(np.random.standard_normal((D, C)) * 2.0 * a),
            "theta_b": bf(np.random.standard_normal(D) * 0.2),
            "phi_w": bf(np.random.standard_normal((D, C)) * a),
            "phi_b": bf(np.random.standard_normal(D) * 0.1)}


def reference(x, g_w, g_b, theta_w, theta_b, phi_w, phi_b):
    xq = mxq(f64(x).reshape(B, C, N), 1, "e4m3")
    g_x = maxpool(conv1x1(mxq(f64(g_w), 1, "e4m3"), f64(g_b), xq)).reshape(B, D, NP)
    theta_x = conv1x1(mxq(f64(theta_w), 1, "e4m3"), f64(theta_b), xq).reshape(B, D, N)
    phi_x = maxpool(conv1x1(mxq(f64(phi_w), 1, "e4m3"), f64(phi_b), xq)).reshape(B, D, NP)
    return g_x, theta_x, phi_x

@@ -1,0 +1,212 @@
+from contextlib import ExitStack
+
+import concourse.mybir as mybir
+from concourse.masks import make_identity
+
+BF16 = mybir.dt.bfloat16
+F32 = mybir.dt.float32
+U32 = mybir.dt.uint32
+U8 = mybir.dt.uint8
+FP8X4 = mybir.dt.float8_e4m3fn_x4
+IDENTITY = mybir.ActivationFunctionType.Identity
+ALU = mybir.AluOpType
+
+P = 128
+PACK = 4
+PAIR = 2
+K_PASS = P * PACK
+CHANNELS = 1024
+PASSES = CHANNELS // K_PASS
+OUT_CHANNELS = 512
+O_TILES = OUT_CHANNELS // P
+WIDTH = 16
+POSITIONS = 8 * 16 * WIDTH
+CHUNK = 512
+CHUNKS = POSITIONS // CHUNK
+WINDOW = 2
+POOLED_CHUNK = CHUNK // (WINDOW * WINDOW)
+STORE_CHUNKS = 2
+G, PHI, THETA = 0, 1, 2
+VECTOR_COLUMNS_FIRST = 384
+VECTOR_COLUMNS_LATER = 128
+
+FLOPS = 2 * 3 * OUT_CHANNELS * CHANNELS * POSITIONS
+
+
+def tile_nonlocalblocknd_pa_kernel(
+    tc, x, g_w, g_b, theta_w, theta_b, phi_w, phi_b, out_0, out_1, out_2
+):
+    nc = tc.nc
+    weights = {G: g_w, PHI: phi_w, THETA: theta_w}
+    biases = {G: g_b, PHI: phi_b, THETA: theta_b}
+    x_rows = x.rearrange("b c t h w -> (b c) (t h w)")
+    outs = {
+        G: out_0.rearrange("b (p a) n -> (b p) a n", a=O_TILES),
+        PHI: out_2.rearrange("b (p a) n -> (b p) a n", a=O_TILES),
+        THETA: out_1.rearrange("b (p a) n -> (b p) a n", a=O_TILES),
+    }
+
+    with ExitStack() as ctx:
+        keep = ctx.enter_context(tc.tile_pool(name="keep", bufs=1))
+        results = ctx.enter_context(tc.tile_pool(name="results", bufs=4))
+        psum = ctx.enter_context(tc.psum_pool(name="psum", bufs=8))
+        ctx.enter_context(tc.manual_schedule())
+
+        w_raw = [keep.tile([P, O_TILES, CHANNELS], BF16, name="w_raw%d" % k) for k in range(3)]
+        w_grouped = [
+            keep.tile([P, O_TILES, PASSES * P * PACK], BF16, name="w_grouped%d" % k, align_bytes=64)
+            for k in range(3)
+        ]
+        w_codes = [
+            keep.tile([P, O_TILES, PASSES, P], U32, name="w_codes%d" % k, align_bytes=64)
+            for k in range(3)
+        ]
+        w_scales = [
+            keep.tile([P, O_TILES, PASSES, P], U8, name="w_scales%d" % k, align_bytes=64)
+            for k in range(3)
+        ]
+        x_raw = [keep.tile([P, PASSES, PACK, CHUNK], BF16, name="x_raw%d" % j) for j in range(CHUNKS)]
+        x_grouped = [
+            keep.tile([P, PASSES, CHUNK, PACK], BF16, name="x_grouped%d" % j, align_bytes=64)
+            for j in range(CHUNKS)
+        ]
+        x_codes = [
+            keep.tile([P, PASSES, CHUNK], U32, name="x_codes%d" % j, align_bytes=64)
+            for j in range(CHUNKS)
+        ]
+        x_scales = [
+            keep.tile([P, PASSES, CHUNK], U8, name="x_scales%d" % j, align_bytes=64)
+            for j in range(CHUNKS)
+        ]
+        bias_bf16 = keep.tile([P, 3, 16], BF16, name="bias_bf16")
+        bias = keep.tile([P, 3, O_TILES], F32, name="bias")
+        identity = keep.tile([P, P], F32, name="identity")
+
+        for k in range(3):
+            nc.scalar.dma_start(
+                out=bias_bf16[:, k, 0:O_TILES],
+                in_=biases[k].rearrange("(p a) -> p a", a=O_TILES),
+            )
+        for k in range(3):
+            nc.sync.dma_start(
+                out=w_raw[k][:], in_=weights[k].rearrange("(p a) c -> p a c", a=O_TILES)
+            )
+        for j in range(CHUNKS):
+            for g in range(PASSES):
+                for u in range(PAIR):
+                    first = K_PASS * g + PAIR * P * u
+                    nc.sync.dma_start(
+                        out=x_raw[j][:, g, PAIR * u : PAIR * u + PAIR, :],
+                        in_=x_rows[
+                            first : first + PAIR * P, CHUNK * j : CHUNK * (j + 1)
+                        ].rearrange("(p e) n -> p e n", e=PAIR),
+                    )
+
+        make_identity(nc, identity[:])
+        nc.vector.tensor_copy(out=bias[:], in_=bias_bf16[:, :, 0:O_TILES])
+
+        for k in range(3):
+            for a in range(O_TILES):
+                words = w_raw[k][:, a, :].bitcast(F32)
+                bank = psum.tile([P, CHUNK], F32, tag="bank")
+                for s in range(PASSES * PAIR):
+                    nc.tensor.transpose(
+                        bank[:, P * s : P * (s + 1)], words[:, P * s : P * (s + 1)], identity[:]
+                    )
+                side_by_side = w_grouped[k][:, a, :].bitcast(F32)
+                copy_out = nc.scalar.copy if a % 2 == 0 else nc.vector.tensor_copy
+                copy_out(
+                    out=side_by_side.rearrange("p (g m u) -> p g m u", g=PASSES, u=PAIR),
+                    in_=bank[:].rearrange("p (g u m) -> p g m u", g=PASSES, u=PAIR),
+                )
+            nc.vector.quantize_mx(
+                out=w_codes[k][:].rearrange("p a g m -> p (a g m)").bitcast(FP8X4),
+                scales=w_scales[k][:].rearrange("p a g m -> p (a g m)"),
+                in_=w_grouped[k][:].rearrange("p a c -> p (a c)"),
+            )
+
+        def regroup(j, g, vector_columns):
+            for copy, columns in (
+                (nc.vector.tensor_copy, slice(0, vector_columns)),
+                (nc.scalar.copy, slice(vector_columns, CHUNK)),
+            ):
+                copy(
+                    out=x_grouped[j][:, g, columns, :].rearrange("p (c i) t -> p c t i", i=4),
+                    in_=x_raw[j][:, g, :, columns].rearrange("p t (c i) -> p c t i", i=4),
+                )
+
+        def quantise(j, g):
+            nc.vector.quantize_mx(
+                out=x_codes[j][:, g, :].bitcast(FP8X4),
+                scales=x_scales[j][:, g, :],
+                in_=x_grouped[j][:, g].rearrange("p n t -> p (n t)"),
+            )
+
+        for g in range(PASSES):
+            regroup(0, g, VECTOR_COLUMNS_FIRST)
+        for g in range(PASSES):
+            quantise(0, g)
+
+        def multiply(j, k, a):
+            acc = psum.tile([P, CHUNK], F32, tag="bank")
+            for g in range(PASSES):
+                nc.tensor.matmul_mx(
+                    out=acc[:],
+                    lhsT=w_codes[k][:, a, g, :].bitcast(FP8X4),
+                    lhsT_scale=w_scales[k][:, a, g, :],
+                    rhs=x_codes[j][:, g, :].bitcast(FP8X4),
+                    rhs_scale=x_scales[j][:, g, :],
+                    start=(g == 0),
+                    stop=(g == PASSES - 1),
+                )
+            return acc
+
+        pooled = {}
+        for j in range(CHUNKS):
+            part = j % STORE_CHUNKS
+            for a in range(O_TILES):
+                if j + 1 < CHUNKS and a < PASSES:
+                    regroup(j + 1, a, VECTOR_COLUMNS_LATER)
+
+                for k in (G, PHI):
+                    acc = multiply(j, k, a)
+                    if part == 0:
+                        pooled[(k, a)] = results.tile(
+                            [P, STORE_CHUNKS * POOLED_CHUNK], F32, name="pooled%d_%d" % (k, a), bufs=2
+                        )
+                    nc.vector.tensor_reduce(
+                        out=pooled[(k, a)][
+                            :, POOLED_CHUNK * part : POOLED_CHUNK * (part + 1)
+                        ].rearrange("p (r v) -> p r v", v=WIDTH // WINDOW),
+                        in_=acc[:].rearrange(
+                            "p (r hp v wp) -> p r v hp wp", hp=WINDOW, v=WIDTH // WINDOW, wp=WINDOW
+                        ),
+                        axis=mybir.AxisListType.XY,
+                        op=ALU.max,
+                    )
+                    if part == STORE_CHUNKS - 1:
+                        nc.gpsimd.tensor_scalar(
+                            out=pooled[(k, a)][:],
+                            in0=pooled[(k, a)][:],
+                            scalar1=1.0,
+                            scalar2=bias[:, k, a : a + 1],
+                            op0=ALU.mult,
+                            op1=ALU.add,
+                        )
+                        last = POOLED_CHUNK * (j + 1)
+                        nc.sync.dma_start(
+                            out=outs[k][:, a, last - STORE_CHUNKS * POOLED_CHUNK : last],
+                            in_=pooled[(k, a)][:],
+                        )
+
+                acc = multiply(j, THETA, a)
+                theta_tile = results.tile([P, CHUNK], F32)
+                nc.scalar.activation(
+                    out=theta_tile[:], in_=acc[:], func=IDENTITY, bias=bias[:, THETA, a : a + 1], scale=1.0
+                )
+                nc.sync.dma_start(
+                    out=outs[THETA][:, a, CHUNK * j : CHUNK * (j + 1)], in_=theta_tile[:]
+                )
+
+                if j + 1 < CHUNKS and 1 <= a <= PASSES:
+                    quantise(j + 1, a - 1)

@@ -87,11 +87,12 @@ def tile_nonlocalblocknd_pa_kernel(
                 out=bias_bf16[:, k, 0:O_TILES],
                 in_=biases[k].rearrange("(p a) -> p a", a=O_TILES),
             )
-        for k in range(3):
+        def load_weights(k):
             nc.sync.dma_start(
                 out=w_raw[k][:], in_=weights[k].rearrange("(p a) c -> p a c", a=O_TILES)
             )
-        for j in range(CHUNKS):
+
+        def load_x(j):
             for g in range(PASSES):
                 for u in range(PAIR):
                     first = K_PASS * g + PAIR * P * u
@@ -102,10 +103,16 @@ def tile_nonlocalblocknd_pa_kernel(
                         ].rearrange("(p e) n -> p e n", e=PAIR),
                     )
 
-        make_identity(nc, identity[:])
-        nc.vector.tensor_copy(out=bias[:], in_=bias_bf16[:, :, 0:O_TILES])
+        load_weights(G)
+        load_weights(PHI)
+        load_x(0)
+        load_weights(THETA)
+        for j in range(1, CHUNKS):
+            load_x(j)
 
-        for k in range(3):
+        make_identity(nc, identity[:])
+
+        def prepare_weights(k):
             for a in range(O_TILES):
                 words = w_raw[k][:, a, :].bitcast(F32)
                 bank = psum.tile([P, CHUNK], F32, tag="bank")
@@ -114,38 +121,40 @@ def tile_nonlocalblocknd_pa_kernel(
                         bank[:, P * s : P * (s + 1)], words[:, P * s : P * (s + 1)], identity[:]
                     )
                 side_by_side = w_grouped[k][:, a, :].bitcast(F32)
-                copy_out = nc.scalar.copy if a % 2 == 0 else nc.vector.tensor_copy
-                copy_out(
+                nc.scalar.copy(
                     out=side_by_side.rearrange("p (g m u) -> p g m u", g=PASSES, u=PAIR),
                     in_=bank[:].rearrange("p (g u m) -> p g m u", g=PASSES, u=PAIR),
                 )
-            nc.vector.quantize_mx(
-                out=w_codes[k][:].rearrange("p a g m -> p (a g m)").bitcast(FP8X4),
-                scales=w_scales[k][:].rearrange("p a g m -> p (a g m)"),
-                in_=w_grouped[k][:].rearrange("p a c -> p (a c)"),
-            )
+                if a % 2 == 1:
+                    two = slice(a - 1, a + 1)
+                    nc.vector.quantize_mx(
+                        out=w_codes[k][:, two].rearrange("p a g m -> p (a g m)").bitcast(FP8X4),
+                        scales=w_scales[k][:, two].rearrange("p a g m -> p (a g m)"),
+                        in_=w_grouped[k][:, two].rearrange("p a c -> p (a c)"),
+                    )
 
-        def regroup(j, g, vector_columns):
-            for copy, columns in (
-                (nc.vector.tensor_copy, slice(0, vector_columns)),
-                (nc.scalar.copy, slice(vector_columns, CHUNK)),
-            ):
-                copy(
-                    out=x_grouped[j][:, g, columns, :].rearrange("p (c i) t -> p c t i", i=4),
-                    in_=x_raw[j][:, g, :, columns].rearrange("p t (c i) -> p c t i", i=4),
+        def prepare_x(j, vector_columns):
+            for g in range(PASSES):
+                for copy, columns in (
+                    (nc.vector.tensor_copy, slice(0, vector_columns)),
+                    (nc.scalar.copy, slice(vector_columns, CHUNK)),
+                ):
+                    copy(
+                        out=x_grouped[j][:, g, columns, :].rearrange("p (c i) t -> p c t i", i=4),
+                        in_=x_raw[j][:, g, :, columns].rearrange("p t (c i) -> p c t i", i=4),
+                    )
+            for g in range(PASSES):
+                nc.vector.quantize_mx(
+                    out=x_codes[j][:, g, :].bitcast(FP8X4),
+                    scales=x_scales[j][:, g, :],
+                    in_=x_grouped[j][:, g].rearrange("p n t -> p (n t)"),
                 )
 
-        def quantise(j, g):
-            nc.vector.quantize_mx(
-                out=x_codes[j][:, g, :].bitcast(FP8X4),
-                scales=x_scales[j][:, g, :],
-                in_=x_grouped[j][:, g].rearrange("p n t -> p (n t)"),
-            )
-
-        for g in range(PASSES):
-            regroup(0, g, VECTOR_COLUMNS_FIRST)
-        for g in range(PASSES):
-            quantise(0, g)
+        prepare_weights(G)
+        prepare_weights(PHI)
+        prepare_x(0, VECTOR_COLUMNS_FIRST)
+        prepare_weights(THETA)
+        nc.vector.tensor_copy(out=bias[:], in_=bias_bf16[:, :, 0:O_TILES])
 
         def multiply(j, k, a):
             acc = psum.tile([P, CHUNK], F32, tag="bank")
@@ -162,51 +171,51 @@ def tile_nonlocalblocknd_pa_kernel(
             return acc
 
         pooled = {}
-        for j in range(CHUNKS):
+
+        def pool_and_store(j, k, a, acc):
             part = j % STORE_CHUNKS
-            for a in range(O_TILES):
-                if j + 1 < CHUNKS and a < PASSES:
-                    regroup(j + 1, a, VECTOR_COLUMNS_LATER)
-
-                for k in (G, PHI):
-                    acc = multiply(j, k, a)
-                    if part == 0:
-                        pooled[(k, a)] = results.tile(
-                            [P, STORE_CHUNKS * POOLED_CHUNK], F32, name="pooled%d_%d" % (k, a), bufs=2
-                        )
-                    nc.vector.tensor_reduce(
-                        out=pooled[(k, a)][
-                            :, POOLED_CHUNK * part : POOLED_CHUNK * (part + 1)
-                        ].rearrange("p (r v) -> p r v", v=WIDTH // WINDOW),
-                        in_=acc[:].rearrange(
-                            "p (r hp v wp) -> p r v hp wp", hp=WINDOW, v=WIDTH // WINDOW, wp=WINDOW
-                        ),
-                        axis=mybir.AxisListType.XY,
-                        op=ALU.max,
-                    )
-                    if part == STORE_CHUNKS - 1:
-                        nc.gpsimd.tensor_scalar(
-                            out=pooled[(k, a)][:],
-                            in0=pooled[(k, a)][:],
-                            scalar1=1.0,
-                            scalar2=bias[:, k, a : a + 1],
-                            op0=ALU.mult,
-                            op1=ALU.add,
-                        )
-                        last = POOLED_CHUNK * (j + 1)
-                        nc.sync.dma_start(
-                            out=outs[k][:, a, last - STORE_CHUNKS * POOLED_CHUNK : last],
-                            in_=pooled[(k, a)][:],
-                        )
-
-                acc = multiply(j, THETA, a)
-                theta_tile = results.tile([P, CHUNK], F32)
-                nc.scalar.activation(
-                    out=theta_tile[:], in_=acc[:], func=IDENTITY, bias=bias[:, THETA, a : a + 1], scale=1.0
+            if part == 0:
+                pooled[(k, a)] = results.tile(
+                    [P, STORE_CHUNKS * POOLED_CHUNK], F32, name="pooled%d_%d" % (k, a), bufs=2
                 )
+            nc.vector.tensor_reduce(
+                out=pooled[(k, a)][:, POOLED_CHUNK * part : POOLED_CHUNK * (part + 1)].rearrange(
+                    "p (r v) -> p r v", v=WIDTH // WINDOW
+                ),
+                in_=acc[:].rearrange(
+                    "p (r hp v wp) -> p r v hp wp", hp=WINDOW, v=WIDTH // WINDOW, wp=WINDOW
+                ),
+                axis=mybir.AxisListType.XY,
+                op=ALU.max,
+            )
+            if part == STORE_CHUNKS - 1:
+                nc.gpsimd.tensor_scalar(
+                    out=pooled[(k, a)][:],
+                    in0=pooled[(k, a)][:],
+                    scalar1=1.0,
+                    scalar2=bias[:, k, a : a + 1],
+                    op0=ALU.mult,
+                    op1=ALU.add,
+                )
+                last = POOLED_CHUNK * (j + 1)
                 nc.sync.dma_start(
-                    out=outs[THETA][:, a, CHUNK * j : CHUNK * (j + 1)], in_=theta_tile[:]
+                    out=outs[k][:, a, last - STORE_CHUNKS * POOLED_CHUNK : last],
+                    in_=pooled[(k, a)][:],
                 )
 
-                if j + 1 < CHUNKS and 1 <= a <= PASSES:
-                    quantise(j + 1, a - 1)
+        def add_bias_and_store(j, a, acc):
+            theta_tile = results.tile([P, CHUNK], F32)
+            nc.scalar.activation(
+                out=theta_tile[:], in_=acc[:], func=IDENTITY, bias=bias[:, THETA, a : a + 1], scale=1.0
+            )
+            nc.sync.dma_start(out=outs[THETA][:, a, CHUNK * j : CHUNK * (j + 1)], in_=theta_tile[:])
+
+        for j in range(CHUNKS):
+            for a in range(O_TILES):
+                pool_and_store(j, G, a, multiply(j, G, a))
+            if j + 1 < CHUNKS:
+                prepare_x(j + 1, VECTOR_COLUMNS_LATER)
+            for a in range(O_TILES):
+                pool_and_store(j, PHI, a, multiply(j, PHI, a))
+            for a in range(O_TILES):
+                add_bias_and_store(j, a, multiply(j, THETA, a))

@@ -88,9 +88,9 @@ def tile_nonlocalblocknd_pa_kernel(
                 in_=biases[k].rearrange("(p a) -> p a", a=O_TILES),
             )
         def load_weights(k):
-            nc.sync.dma_start(
-                out=w_raw[k][:], in_=weights[k].rearrange("(p a) c -> p a c", a=O_TILES)
-            )
+            rows = weights[k].rearrange("(p a) c -> p a c", a=O_TILES)
+            for two in (slice(0, 2), slice(2, 4)):
+                nc.sync.dma_start(out=w_raw[k][:, two, :], in_=rows[:, two, :])
 
         def load_x(j):
             for g in range(PASSES):
@@ -151,8 +151,8 @@ def tile_nonlocalblocknd_pa_kernel(
                 )
 
         prepare_weights(G)
-        prepare_weights(PHI)
         prepare_x(0, VECTOR_COLUMNS_FIRST)
+        prepare_weights(PHI)
         prepare_weights(THETA)
         nc.vector.tensor_copy(out=bias[:], in_=bias_bf16[:, :, 0:O_TILES])
 

@@ -27,8 +27,8 @@ WINDOW = 2
 POOLED_CHUNK = CHUNK // (WINDOW * WINDOW)
 STORE_CHUNKS = 2
 G, PHI, THETA = 0, 1, 2
-VECTOR_COLUMNS_FIRST = 384
-VECTOR_COLUMNS_LATER = 128
+VECTOR_COLUMNS = 384
+GPSIMD_COLUMNS = 128
 
 FLOPS = 2 * 3 * OUT_CHANNELS * CHANNELS * POSITIONS
 
@@ -133,16 +133,23 @@ def tile_nonlocalblocknd_pa_kernel(
                         in_=w_grouped[k][:, two].rearrange("p a c -> p (a c)"),
                     )
 
-        def prepare_x(j, vector_columns):
+        def gpsimd_copy(out, in_):
+            nc.gpsimd.tensor_scalar(
+                out=out, in0=in_, scalar1=1.0, scalar2=0.0, op0=ALU.mult, op1=ALU.add
+            )
+
+        def regroup(j, helper_copy, helper_columns):
             for g in range(PASSES):
                 for copy, columns in (
-                    (nc.vector.tensor_copy, slice(0, vector_columns)),
-                    (nc.scalar.copy, slice(vector_columns, CHUNK)),
+                    (helper_copy, slice(0, helper_columns)),
+                    (nc.scalar.copy, slice(helper_columns, CHUNK)),
                 ):
                     copy(
                         out=x_grouped[j][:, g, columns, :].rearrange("p (c i) t -> p c t i", i=4),
                         in_=x_raw[j][:, g, :, columns].rearrange("p t (c i) -> p c t i", i=4),
                     )
+
+        def quantise(j):
             for g in range(PASSES):
                 nc.vector.quantize_mx(
                     out=x_codes[j][:, g, :].bitcast(FP8X4),
@@ -151,7 +158,8 @@ def tile_nonlocalblocknd_pa_kernel(
                 )
 
         prepare_weights(G)
-        prepare_x(0, VECTOR_COLUMNS_FIRST)
+        regroup(0, nc.vector.tensor_copy, VECTOR_COLUMNS)
+        quantise(0)
         prepare_weights(PHI)
         prepare_weights(THETA)
         nc.vector.tensor_copy(out=bias[:], in_=bias_bf16[:, :, 0:O_TILES])
@@ -211,10 +219,12 @@ def tile_nonlocalblocknd_pa_kernel(
             nc.sync.dma_start(out=outs[THETA][:, a, CHUNK * j : CHUNK * (j + 1)], in_=theta_tile[:])
 
         for j in range(CHUNKS):
+            if j + 1 < CHUNKS:
+                regroup(j + 1, gpsimd_copy, GPSIMD_COLUMNS)
             for a in range(O_TILES):
                 pool_and_store(j, G, a, multiply(j, G, a))
             if j + 1 < CHUNKS:
-                prepare_x(j + 1, VECTOR_COLUMNS_LATER)
+                quantise(j + 1)
             for a in range(O_TILES):
                 pool_and_store(j, PHI, a, multiply(j, PHI, a))
             for a in range(O_TILES):

@@ -212,7 +212,7 @@ def tile_nonlocalblocknd_pa_kernel(
                 )
 
         def add_bias_and_store(j, a, acc):
-            theta_tile = results.tile([P, CHUNK], F32)
+            theta_tile = results.tile([P, CHUNK], F32, bufs=2 * O_TILES)
             nc.scalar.activation(
                 out=theta_tile[:], in_=acc[:], func=IDENTITY, bias=bias[:, THETA, a : a + 1], scale=1.0
             )
@@ -221,11 +221,15 @@ def tile_nonlocalblocknd_pa_kernel(
         for j in range(CHUNKS):
             if j + 1 < CHUNKS:
                 regroup(j + 1, gpsimd_copy, GPSIMD_COLUMNS)
+            if j == CHUNKS - 1:
+                for a in range(O_TILES):
+                    add_bias_and_store(j, a, multiply(j, THETA, a))
             for a in range(O_TILES):
                 pool_and_store(j, G, a, multiply(j, G, a))
             if j + 1 < CHUNKS:
                 quantise(j + 1)
             for a in range(O_TILES):
                 pool_and_store(j, PHI, a, multiply(j, PHI, a))
-            for a in range(O_TILES):
-                add_bias_and_store(j, a, multiply(j, THETA, a))
+            if j + 1 < CHUNKS:
+                for a in range(O_TILES):
+                    add_bias_and_store(j, a, multiply(j, THETA, a))

@@ -29,6 +29,7 @@ STORE_CHUNKS = 2
 G, PHI, THETA = 0, 1, 2
 VECTOR_COLUMNS = 384
 GPSIMD_COLUMNS = 128
+SECOND_CHUNK_VECTOR_COLUMNS = 128
 
 FLOPS = 2 * 3 * OUT_CHANNELS * CHANNELS * POSITIONS
 
@@ -112,8 +113,8 @@ def tile_nonlocalblocknd_pa_kernel(
 
         make_identity(nc, identity[:])
 
-        def prepare_weights(k):
-            for a in range(O_TILES):
+        def turn_weights(k, tiles):
+            for a in tiles:
                 words = w_raw[k][:, a, :].bitcast(F32)
                 bank = psum.tile([P, CHUNK], F32, tag="bank")
                 for s in range(PASSES * PAIR):
@@ -125,13 +126,18 @@ def tile_nonlocalblocknd_pa_kernel(
                     out=side_by_side.rearrange("p (g m u) -> p g m u", g=PASSES, u=PAIR),
                     in_=bank[:].rearrange("p (g u m) -> p g m u", g=PASSES, u=PAIR),
                 )
-                if a % 2 == 1:
-                    two = slice(a - 1, a + 1)
-                    nc.vector.quantize_mx(
-                        out=w_codes[k][:, two].rearrange("p a g m -> p (a g m)").bitcast(FP8X4),
-                        scales=w_scales[k][:, two].rearrange("p a g m -> p (a g m)"),
-                        in_=w_grouped[k][:, two].rearrange("p a c -> p (a c)"),
-                    )
+
+        def quantise_weights(k, two):
+            nc.vector.quantize_mx(
+                out=w_codes[k][:, two].rearrange("p a g m -> p (a g m)").bitcast(FP8X4),
+                scales=w_scales[k][:, two].rearrange("p a g m -> p (a g m)"),
+                in_=w_grouped[k][:, two].rearrange("p a c -> p (a c)"),
+            )
+
+        def prepare_weights(k, pairs=(0, 1)):
+            for pair in pairs:
+                turn_weights(k, (2 * pair, 2 * pair + 1))
+                quantise_weights(k, slice(2 * pair, 2 * pair + 2))
 
         def gpsimd_copy(out, in_):
             nc.gpsimd.tensor_scalar(
@@ -149,6 +155,12 @@ def tile_nonlocalblocknd_pa_kernel(
                         in_=x_raw[j][:, g, :, columns].rearrange("p t (c i) -> p c t i", i=4),
                     )
 
+        def regroup_part(j, g, copy, columns):
+            copy(
+                out=x_grouped[j][:, g, columns, :].rearrange("p (c i) t -> p c t i", i=4),
+                in_=x_raw[j][:, g, :, columns].rearrange("p t (c i) -> p c t i", i=4),
+            )
+
         def quantise(j):
             for g in range(PASSES):
                 nc.vector.quantize_mx(
@@ -158,10 +170,30 @@ def tile_nonlocalblocknd_pa_kernel(
                 )
 
         prepare_weights(G)
+        turn_weights(PHI, (0, 1))
         regroup(0, nc.vector.tensor_copy, VECTOR_COLUMNS)
         quantise(0)
-        prepare_weights(PHI)
-        prepare_weights(THETA)
+        quantise_weights(PHI, slice(0, 2))
+        prepare_weights(PHI, (1,))
+        second_chunk_on_vector = slice(GPSIMD_COLUMNS, GPSIMD_COLUMNS + SECOND_CHUNK_VECTOR_COLUMNS)
+
+        warm = psum.tile([P, CHUNK], F32, tag="bank")
+
+        def keep_clock(moving):
+            nc.tensor.matmul(
+                out=warm[:], lhsT=w_raw[G][:, 0, 0:P], rhs=moving, start=True, stop=True
+            )
+
+        for g in range(PASSES):
+            for u in range(PAIR):
+                keep_clock(x_raw[0][:, g, PAIR * u, :])
+        keep_clock(w_raw[THETA][:, 0, 0:CHUNK])
+        for pair in range(PASSES):
+            regroup_part(1, pair, nc.vector.tensor_copy, second_chunk_on_vector)
+            prepare_weights(THETA, (pair,))
+            if pair == 0:
+                keep_clock(w_raw[THETA][:, 0, 0:CHUNK])
+                keep_clock(w_raw[THETA][:, 1, 0:CHUNK])
         nc.vector.tensor_copy(out=bias[:], in_=bias_bf16[:, :, 0:O_TILES])
 
         def multiply(j, k, a):
@@ -197,14 +229,23 @@ def tile_nonlocalblocknd_pa_kernel(
                 op=ALU.max,
             )
             if part == STORE_CHUNKS - 1:
-                nc.gpsimd.tensor_scalar(
-                    out=pooled[(k, a)][:],
-                    in0=pooled[(k, a)][:],
-                    scalar1=1.0,
-                    scalar2=bias[:, k, a : a + 1],
-                    op0=ALU.mult,
-                    op1=ALU.add,
-                )
+                if (j, k, a) == (CHUNKS - 1, PHI, O_TILES - 1):
+                    nc.vector.tensor_scalar(
+                        out=pooled[(k, a)][:],
+                        in0=pooled[(k, a)][:],
+                        scalar1=bias[:, k, a : a + 1],
+                        scalar2=None,
+                        op0=ALU.add,
+                    )
+                else:
+                    nc.gpsimd.tensor_scalar(
+                        out=pooled[(k, a)][:],
+                        in0=pooled[(k, a)][:],
+                        scalar1=1.0,
+                        scalar2=bias[:, k, a : a + 1],
+                        op0=ALU.mult,
+                        op1=ALU.add,
+                    )
                 last = POOLED_CHUNK * (j + 1)
                 nc.sync.dma_start(
                     out=outs[k][:, a, last - STORE_CHUNKS * POOLED_CHUNK : last],
@@ -219,7 +260,11 @@ def tile_nonlocalblocknd_pa_kernel(
             nc.sync.dma_start(out=outs[THETA][:, a, CHUNK * j : CHUNK * (j + 1)], in_=theta_tile[:])
 
         for j in range(CHUNKS):
-            if j + 1 < CHUNKS:
+            if j == 0:
+                for g in range(PASSES):
+                    regroup_part(1, g, gpsimd_copy, slice(0, GPSIMD_COLUMNS))
+                    regroup_part(1, g, nc.scalar.copy, slice(second_chunk_on_vector.stop, CHUNK))
+            elif j + 1 < CHUNKS:
                 regroup(j + 1, gpsimd_copy, GPSIMD_COLUMNS)
             if j == CHUNKS - 1:
                 for a in range(O_TILES):

from contextlib import ExitStack

import concourse.mybir as mybir
from concourse.masks import make_identity

BF16 = mybir.dt.bfloat16
F32 = mybir.dt.float32
U32 = mybir.dt.uint32
U8 = mybir.dt.uint8
FP8X4 = mybir.dt.float8_e4m3fn_x4
IDENTITY = mybir.ActivationFunctionType.Identity
ALU = mybir.AluOpType

P = 128
PACK = 4
PAIR = 2
K_PASS = P * PACK
CHANNELS = 1024
PASSES = CHANNELS // K_PASS
OUT_CHANNELS = 512
O_TILES = OUT_CHANNELS // P
WIDTH = 16
POSITIONS = 8 * 16 * WIDTH
CHUNK = 512
CHUNKS = POSITIONS // CHUNK
WINDOW = 2
POOLED_CHUNK = CHUNK // (WINDOW * WINDOW)
STORE_CHUNKS = 2
G, PHI, THETA = 0, 1, 2
VECTOR_COLUMNS = 384
GPSIMD_COLUMNS = 128
SECOND_CHUNK_VECTOR_COLUMNS = 128

FLOPS = 2 * 3 * OUT_CHANNELS * CHANNELS * POSITIONS


def tile_nonlocalblocknd_pa_kernel(
    tc, x, g_w, g_b, theta_w, theta_b, phi_w, phi_b, out_0, out_1, out_2
):
    nc = tc.nc
    weights = {G: g_w, PHI: phi_w, THETA: theta_w}
    biases = {G: g_b, PHI: phi_b, THETA: theta_b}
    x_rows = x.rearrange("b c t h w -> (b c) (t h w)")
    outs = {
        G: out_0.rearrange("b (p a) n -> (b p) a n", a=O_TILES),
        PHI: out_2.rearrange("b (p a) n -> (b p) a n", a=O_TILES),
        THETA: out_1.rearrange("b (p a) n -> (b p) a n", a=O_TILES),
    }

    with ExitStack() as ctx:
        keep = ctx.enter_context(tc.tile_pool(name="keep", bufs=1))
        results = ctx.enter_context(tc.tile_pool(name="results", bufs=4))
        psum = ctx.enter_context(tc.psum_pool(name="psum", bufs=8))
        ctx.enter_context(tc.manual_schedule())

        w_raw = [keep.tile([P, O_TILES, CHANNELS], BF16, name="w_raw%d" % k) for k in range(3)]
        w_grouped = [
            keep.tile([P, O_TILES, PASSES * P * PACK], BF16, name="w_grouped%d" % k, align_bytes=64)
            for k in range(3)
        ]
        w_codes = [
            keep.tile([P, O_TILES, PASSES, P], U32, name="w_codes%d" % k, align_bytes=64)
            for k in range(3)
        ]
        w_scales = [
            keep.tile([P, O_TILES, PASSES, P], U8, name="w_scales%d" % k, align_bytes=64)
            for k in range(3)
        ]
        x_raw = [keep.tile([P, PASSES, PACK, CHUNK], BF16, name="x_raw%d" % j) for j in range(CHUNKS)]
        x_grouped = [
            keep.tile([P, PASSES, CHUNK, PACK], BF16, name="x_grouped%d" % j, align_bytes=64)
            for j in range(CHUNKS)
        ]
        x_codes = [
            keep.tile([P, PASSES, CHUNK], U32, name="x_codes%d" % j, align_bytes=64)
            for j in range(CHUNKS)
        ]
        x_scales = [
            keep.tile([P, PASSES, CHUNK], U8, name="x_scales%d" % j, align_bytes=64)
            for j in range(CHUNKS)
        ]
        bias_bf16 = keep.tile([P, 3, 16], BF16, name="bias_bf16")
        bias = keep.tile([P, 3, O_TILES], F32, name="bias")
        identity = keep.tile([P, P], F32, name="identity")

        for k in range(3):
            nc.scalar.dma_start(
                out=bias_bf16[:, k, 0:O_TILES],
                in_=biases[k].rearrange("(p a) -> p a", a=O_TILES),
            )
        def load_weights(k):
            rows = weights[k].rearrange("(p a) c -> p a c", a=O_TILES)
            for two in (slice(0, 2), slice(2, 4)):
                nc.sync.dma_start(out=w_raw[k][:, two, :], in_=rows[:, two, :])

        def load_x(j):
            for g in range(PASSES):
                for u in range(PAIR):
                    first = K_PASS * g + PAIR * P * u
                    nc.sync.dma_start(
                        out=x_raw[j][:, g, PAIR * u : PAIR * u + PAIR, :],
                        in_=x_rows[
                            first : first + PAIR * P, CHUNK * j : CHUNK * (j + 1)
                        ].rearrange("(p e) n -> p e n", e=PAIR),
                    )

        load_weights(G)
        load_weights(PHI)
        load_x(0)
        load_weights(THETA)
        for j in range(1, CHUNKS):
            load_x(j)

        make_identity(nc, identity[:])

        def turn_weights(k, tiles):
            for a in tiles:
                words = w_raw[k][:, a, :].bitcast(F32)
                bank = psum.tile([P, CHUNK], F32, tag="bank")
                for s in range(PASSES * PAIR):
                    nc.tensor.transpose(
                        bank[:, P * s : P * (s + 1)], words[:, P * s : P * (s + 1)], identity[:]
                    )
                side_by_side = w_grouped[k][:, a, :].bitcast(F32)
                nc.scalar.copy(
                    out=side_by_side.rearrange("p (g m u) -> p g m u", g=PASSES, u=PAIR),
                    in_=bank[:].rearrange("p (g u m) -> p g m u", g=PASSES, u=PAIR),
                )

        def quantise_weights(k, two):
            nc.vector.quantize_mx(
                out=w_codes[k][:, two].rearrange("p a g m -> p (a g m)").bitcast(FP8X4),
                scales=w_scales[k][:, two].rearrange("p a g m -> p (a g m)"),
                in_=w_grouped[k][:, two].rearrange("p a c -> p (a c)"),
            )

        def prepare_weights(k, pairs=(0, 1)):
            for pair in pairs:
                turn_weights(k, (2 * pair, 2 * pair + 1))
                quantise_weights(k, slice(2 * pair, 2 * pair + 2))

        def gpsimd_copy(out, in_):
            nc.gpsimd.tensor_scalar(
                out=out, in0=in_, scalar1=1.0, scalar2=0.0, op0=ALU.mult, op1=ALU.add
            )

        def regroup(j, helper_copy, helper_columns):
            for g in range(PASSES):
                for copy, columns in (
                    (helper_copy, slice(0, helper_columns)),
                    (nc.scalar.copy, slice(helper_columns, CHUNK)),
                ):
                    copy(
                        out=x_grouped[j][:, g, columns, :].rearrange("p (c i) t -> p c t i", i=4),
                        in_=x_raw[j][:, g, :, columns].rearrange("p t (c i) -> p c t i", i=4),
                    )

        def regroup_part(j, g, copy, columns):
            copy(
                out=x_grouped[j][:, g, columns, :].rearrange("p (c i) t -> p c t i", i=4),
                in_=x_raw[j][:, g, :, columns].rearrange("p t (c i) -> p c t i", i=4),
            )

        def quantise(j):
            for g in range(PASSES):
                nc.vector.quantize_mx(
                    out=x_codes[j][:, g, :].bitcast(FP8X4),
                    scales=x_scales[j][:, g, :],
                    in_=x_grouped[j][:, g].rearrange("p n t -> p (n t)"),
                )

        prepare_weights(G)
        turn_weights(PHI, (0, 1))
        regroup(0, nc.vector.tensor_copy, VECTOR_COLUMNS)
        quantise(0)
        quantise_weights(PHI, slice(0, 2))
        prepare_weights(PHI, (1,))
        second_chunk_on_vector = slice(GPSIMD_COLUMNS, GPSIMD_COLUMNS + SECOND_CHUNK_VECTOR_COLUMNS)

        warm = psum.tile([P, CHUNK], F32, tag="bank")

        def keep_clock(moving):
            nc.tensor.matmul(
                out=warm[:], lhsT=w_raw[G][:, 0, 0:P], rhs=moving, start=True, stop=True
            )

        for g in range(PASSES):
            for u in range(PAIR):
                keep_clock(x_raw[0][:, g, PAIR * u, :])
        keep_clock(w_raw[THETA][:, 0, 0:CHUNK])
        for pair in range(PASSES):
            regroup_part(1, pair, nc.vector.tensor_copy, second_chunk_on_vector)
            prepare_weights(THETA, (pair,))
            if pair == 0:
                keep_clock(w_raw[THETA][:, 0, 0:CHUNK])
                keep_clock(w_raw[THETA][:, 1, 0:CHUNK])
        nc.vector.tensor_copy(out=bias[:], in_=bias_bf16[:, :, 0:O_TILES])

        def multiply(j, k, a):
            acc = psum.tile([P, CHUNK], F32, tag="bank")
            for g in range(PASSES):
                nc.tensor.matmul_mx(
                    out=acc[:],
                    lhsT=w_codes[k][:, a, g, :].bitcast(FP8X4),
                    lhsT_scale=w_scales[k][:, a, g, :],
                    rhs=x_codes[j][:, g, :].bitcast(FP8X4),
                    rhs_scale=x_scales[j][:, g, :],
                    start=(g == 0),
                    stop=(g == PASSES - 1),
                )
            return acc

        pooled = {}

        def pool_and_store(j, k, a, acc):
            part = j % STORE_CHUNKS
            if part == 0:
                pooled[(k, a)] = results.tile(
                    [P, STORE_CHUNKS * POOLED_CHUNK], F32, name="pooled%d_%d" % (k, a), bufs=2
                )
            nc.vector.tensor_reduce(
                out=pooled[(k, a)][:, POOLED_CHUNK * part : POOLED_CHUNK * (part + 1)].rearrange(
                    "p (r v) -> p r v", v=WIDTH // WINDOW
                ),
                in_=acc[:].rearrange(
                    "p (r hp v wp) -> p r v hp wp", hp=WINDOW, v=WIDTH // WINDOW, wp=WINDOW
                ),
                axis=mybir.AxisListType.XY,
                op=ALU.max,
            )
            if part == STORE_CHUNKS - 1:
                if (j, k, a) == (CHUNKS - 1, PHI, O_TILES - 1):
                    nc.vector.tensor_scalar(
                        out=pooled[(k, a)][:],
                        in0=pooled[(k, a)][:],
                        scalar1=bias[:, k, a : a + 1],
                        scalar2=None,
                        op0=ALU.add,
                    )
                else:
                    nc.gpsimd.tensor_scalar(
                        out=pooled[(k, a)][:],
                        in0=pooled[(k, a)][:],
                        scalar1=1.0,
                        scalar2=bias[:, k, a : a + 1],
                        op0=ALU.mult,
                        op1=ALU.add,
                    )
                last = POOLED_CHUNK * (j + 1)
                nc.sync.dma_start(
                    out=outs[k][:, a, last - STORE_CHUNKS * POOLED_CHUNK : last],
                    in_=pooled[(k, a)][:],
                )

        def add_bias_and_store(j, a, acc):
            theta_tile = results.tile([P, CHUNK], F32, bufs=2 * O_TILES)
            nc.scalar.activation(
                out=theta_tile[:], in_=acc[:], func=IDENTITY, bias=bias[:, THETA, a : a + 1], scale=1.0
            )
            nc.sync.dma_start(out=outs[THETA][:, a, CHUNK * j : CHUNK * (j + 1)], in_=theta_tile[:])

        for j in range(CHUNKS):
            if j == 0:
                for g in range(PASSES):
                    regroup_part(1, g, gpsimd_copy, slice(0, GPSIMD_COLUMNS))
                    regroup_part(1, g, nc.scalar.copy, slice(second_chunk_on_vector.stop, CHUNK))
            elif j + 1 < CHUNKS:
                regroup(j + 1, gpsimd_copy, GPSIMD_COLUMNS)
            if j == CHUNKS - 1:
                for a in range(O_TILES):
                    add_bias_and_store(j, a, multiply(j, THETA, a))
            for a in range(O_TILES):
                pool_and_store(j, G, a, multiply(j, G, a))
            if j + 1 < CHUNKS:
                quantise(j + 1)
            for a in range(O_TILES):
                pool_and_store(j, PHI, a, multiply(j, PHI, a))
            if j + 1 < CHUNKS:
                for a in range(O_TILES):
                    add_bias_and_store(j, a, multiply(j, THETA, a))
